import numpy as np
import ml_dtypes


def mxq(x, axis, fmt="e4m3"):
    dtype, down = {"e4m3": (ml_dtypes.float8_e4m3fn, 7), "e5m2": (ml_dtypes.float8_e5m2, 14)}[fmt]
    v = np.moveaxis(np.asarray(x, np.float32).astype(ml_dtypes.bfloat16).astype(np.float64), axis, -1)
    blocks = v.reshape(v.shape[:-1] + (-1, 32))
    amax = np.abs(blocks).max(-1, keepdims=True)
    byte = np.maximum(np.where(amax > 0, np.frexp(amax)[1] - 1 + 127, 0) - down, 1)
    scale = np.exp2(byte - 127.0)
    codes = (blocks / scale).astype(np.float32).astype(dtype).astype(np.float64)
    return np.moveaxis((codes * scale).reshape(v.shape), -1, axis)


WIDE = False


def mx_kscale(k):
    if not WIDE:
        return np.ones(k)
    levels = np.array([10, -10, 5, -5, 0])
    a = np.random.permutation(np.resize(levels, k // 512 * 4)).reshape(k // 512, 4)
    idx = np.arange(k)
    return np.exp2(a[idx // 512, idx % 128 // 32])


BF16 = ml_dtypes.bfloat16


def bf(x):
    return np.asarray(x, np.float32).astype(BF16)


def f64(x):
    return np.asarray(x).astype(np.float64)


H, N, S, T, L, K = 2, 2, 256, 2048, 4096, 512
NH = N * H


def rel_shift(p):
    zero_pad = np.zeros((NH, S, 1))
    padded = np.concatenate([zero_pad, p], axis=2)
    padded = padded.reshape(NH, T + 1, S)
    return padded[:, 1:, :].reshape(NH, S, T)


def setup_inputs():
    s = mx_kscale(K)
    return {"queries": bf(np.random.standard_normal((NH, S, K)) * s),
            "v_bias": bf(np.random.standard_normal((1, H, 1, K)) / np.sqrt(K) * s),
            "R": bf(np.random.standard_normal((H, L, K)) / s)}


def reference(queries, v_bias, R):
    q = (f64(queries) * K ** -0.5).reshape(N, H, S, K)
    q_v = q + f64(v_bias)
    r = f64(R)[:, :T, :]
    pos = mxq(q_v, 3, "e4m3") @ mxq(r, 2, "e4m3").transpose(0, 2, 1)
    return rel_shift(pos.reshape(NH, S, T))

@@ -1,0 +1,161 @@
+from contextlib import ExitStack
+
+import concourse.mybir as mybir
+from concourse.masks import make_identity
+
+F32 = mybir.dt.float32
+BF16 = mybir.dt.bfloat16
+U32 = mybir.dt.uint32
+U8 = mybir.dt.uint8
+FP8X4 = mybir.dt.float8_e4m3fn_x4
+MULT = mybir.AluOpType.mult
+ADD = mybir.AluOpType.add
+
+P = 128
+HEADS = 2
+BATCH = 4
+S = 256
+T = 2048
+K = 512
+PACK = 4
+WORDS = K // 2
+S_BLOCKS = S // P
+T_CHUNK = 512
+T_CHUNKS = T // T_CHUNK
+ROWS = T_CHUNK // P
+PAD = 8
+WIDE = T + 1
+DROP = S
+
+FLOPS = 2 * BATCH * S * T * K
+BYTES = 2 * (BATCH * S * K + HEADS * K + HEADS * T * K) + 4 * BATCH * S * T
+
+
+def tile_relativepositionsdpa_pa_kernel(tc, queries, v_bias, R, out):
+    nc = tc.nc
+    with ExitStack() as ctx:
+        keep = ctx.enter_context(tc.tile_pool(name="keep", bufs=1))
+        stage = ctx.enter_context(tc.tile_pool(name="stage", bufs=3))
+        psum = ctx.enter_context(tc.psum_pool(name="psum", bufs=4))
+
+        ident = keep.tile([P, P], F32)
+        make_identity(nc, ident[:])
+        bias_rows = keep.tile([P, K], BF16)
+        nc.vector.memset(bias_rows[:], 0.0)
+        out_rows = [keep.tile([P, PAD + T], F32, name="out_rows%d" % i) for i in range(BATCH * S_BLOCKS)]
+        for rows in out_rows:
+            nc.vector.memset(rows[:, 0:PAD], 0.0)
+
+        nc.sync.dma_start(out=bias_rows[0:HEADS, :], in_=v_bias.rearrange("o h i k -> (o h i) k"))
+        q_raw = [keep.tile([P, S_BLOCKS * K], BF16, name="q_raw%d" % b) for b in range(BATCH)]
+        r_raw = [keep.tile([P, ROWS * K], BF16, name="r_raw%d" % i) for i in range(HEADS * T_CHUNKS)]
+        for h in range(HEADS):
+            for b in range(h, BATCH, HEADS):
+                nc.sync.dma_start(
+                    out=q_raw[b][:].rearrange("p (j k) -> p j k", j=S_BLOCKS),
+                    in_=queries[b].rearrange("(j p) k -> p j k", p=P),
+                )
+            for c in range(T_CHUNKS):
+                nc.sync.dma_start(
+                    out=r_raw[h * T_CHUNKS + c][:],
+                    in_=R[h, c * T_CHUNK : (c + 1) * T_CHUNK, :].rearrange("(p j) k -> p (j k)", j=ROWS),
+                )
+
+        bias_sb = keep.tile([P, HEADS * PACK], BF16)
+        bias_t = psum.tile([P, 2 * P], F32, tag="flip")
+        for u in range(2):
+            nc.tensor.transpose(bias_t[:, u * P : (u + 1) * P], bias_rows[:].bitcast(F32)[:, u * P : (u + 1) * P], ident[:])
+        nc.vector.tensor_copy(
+            out=bias_sb[:].bitcast(F32).rearrange("p (h u) -> p h u", u=2),
+            in_=bias_t[:].rearrange("p (u s) -> p s u", u=2)[:, 0:HEADS, :],
+        )
+
+        q_codes = keep.tile([P, BATCH, S], U32, align_bytes=64)
+        q_scales = keep.tile([P, BATCH, S], U8, align_bytes=64)
+        r_codes = keep.tile([P, HEADS * T_CHUNKS, T_CHUNK], U32, align_bytes=64)
+        r_scales = keep.tile([P, HEADS * T_CHUNKS, T_CHUNK], U8, align_bytes=64)
+
+        def prepare_queries(b):
+            h = b % HEADS
+            words = q_raw[b][:].bitcast(F32)
+            flip = psum.tile([P, 2 * S], F32, tag="flip")
+            for u in range(2):
+                for j in range(S_BLOCKS):
+                    nc.tensor.transpose(
+                        flip[:, u * S + j * P : u * S + (j + 1) * P],
+                        words[:, j * WORDS + u * P : j * WORDS + (u + 1) * P],
+                        ident[:],
+                    )
+            q_pairs = stage.tile([P, S * PACK], BF16)
+            nc.scalar.copy(
+                out=q_pairs[:].bitcast(F32).rearrange("p (s u) -> p s u", u=2),
+                in_=flip[:].rearrange("p (u s) -> p s u", u=2),
+            )
+            q_v = stage.tile([P, S * PACK], BF16, align_bytes=64)
+            nc.vector.scalar_tensor_tensor(
+                out=q_v[:].rearrange("p (s t) -> p s t", t=PACK),
+                in0=q_pairs[:].rearrange("p (s t) -> p s t", t=PACK),
+                scalar=K**-0.5,
+                in1=bias_sb[:, h * PACK : (h + 1) * PACK].unsqueeze(1).to_broadcast([P, S, PACK]),
+                op0=MULT,
+                op1=ADD,
+            )
+            nc.vector.quantize_mx(out=q_codes[:, b, :].bitcast(FP8X4), scales=q_scales[:, b, :], in_=q_v[:])
+
+        def prepare_table(i):
+            words = r_raw[i][:].bitcast(F32)
+            grouped = stage.tile([P, T_CHUNK * PACK], BF16, align_bytes=64)
+            grouped_words = grouped[:].bitcast(F32).rearrange("p (n g f) -> p n g f", g=2, f=4)
+            for g in range(2):
+                flip = psum.tile([P, 4 * P], F32, tag="flip")
+                for f in range(4):
+                    j, u = 2 * g + f // 2, f % 2
+                    nc.tensor.transpose(
+                        flip[:, f * P : (f + 1) * P],
+                        words[:, j * WORDS + u * P : j * WORDS + (u + 1) * P],
+                        ident[:],
+                    )
+                nc.scalar.copy(out=grouped_words[:, :, g, :], in_=flip[:].rearrange("p (f n) -> p n f", f=4))
+            nc.vector.quantize_mx(out=r_codes[:, i, :].bitcast(FP8X4), scales=r_scales[:, i, :], in_=grouped[:])
+
+        def multiply(h, c):
+            i = h * T_CHUNKS + c
+            for b in range(h, BATCH, HEADS):
+                for j in range(S_BLOCKS):
+                    acc = psum.tile([P, T_CHUNK], F32, tag="acc")
+                    nc.tensor.matmul_mx(
+                        out=acc[:],
+                        lhsT=q_codes[:, b, j * P : (j + 1) * P].bitcast(FP8X4),
+                        lhsT_scale=q_scales[:, b, j * P : (j + 1) * P],
+                        rhs=r_codes[:, i, :].bitcast(FP8X4),
+                        rhs_scale=r_scales[:, i, :],
+                        start=True,
+                        stop=True,
+                    )
+                    dst = out_rows[b * S_BLOCKS + j][:, PAD + c * T_CHUNK : PAD + (c + 1) * T_CHUNK]
+                    if j == 0:
+                        nc.vector.tensor_copy(out=dst, in_=acc[:])
+                    else:
+                        nc.scalar.copy(out=dst, in_=acc[:])
+
+        def store(b):
+            flat = out[b].rearrange("s t -> (s t)")
+            first = out_rows[b * S_BLOCKS]
+            cut = flat[0 : P * WIDE].rearrange("(p w) -> p w", w=WIDE)
+            nc.sync.dma_start(out=cut[:, 0 : WIDE - DROP], in_=first[:, PAD - 1 + DROP : PAD + T])
+            nc.sync.dma_start(out=cut[15 : P - 1, WIDE - DROP : WIDE], in_=first[16:P, PAD - 1 : PAD - 1 + DROP])
+            nc.sync.dma_start(out=cut[0:15, WIDE - DROP : WIDE], in_=first[1:16, PAD - 1 : PAD - 1 + DROP])
+            second = out_rows[b * S_BLOCKS + 1]
+            nc.sync.dma_start(
+                out=flat[P * WIDE - DROP : S * T].rearrange("(p w) -> p w", w=WIDE),
+                in_=second[:, PAD - 1 : PAD + T],
+            )
+
+        for h in range(HEADS):
+            for b in range(h, BATCH, HEADS):
+                prepare_queries(b)
+            for c in range(T_CHUNKS):
+                prepare_table(h * T_CHUNKS + c)
+                multiply(h, c)
+            for b in range(h, BATCH, HEADS):
+                store(b)

@@ -13,7 +13,8 @@ ADD = mybir.AluOpType.add
 
 P = 128
 HEADS = 2
-BATCH = 4
+SEQS = 2
+BATCH = SEQS * HEADS
 S = 256
 T = 2048
 K = 512
@@ -50,12 +51,13 @@ def tile_relativepositionsdpa_pa_kernel(tc, queries, v_bias, R, out):
         q_raw = [keep.tile([P, S_BLOCKS * K], BF16, name="q_raw%d" % b) for b in range(BATCH)]
         r_raw = [keep.tile([P, ROWS * K], BF16, name="r_raw%d" % i) for i in range(HEADS * T_CHUNKS)]
         for h in range(HEADS):
-            for b in range(h, BATCH, HEADS):
-                nc.sync.dma_start(
-                    out=q_raw[b][:].rearrange("p (j k) -> p j k", j=S_BLOCKS),
-                    in_=queries[b].rearrange("(j p) k -> p j k", p=P),
-                )
             for c in range(T_CHUNKS):
+                if c < SEQS:
+                    b = c * HEADS + h
+                    nc.sync.dma_start(
+                        out=q_raw[b][:].rearrange("p (j k) -> p j k", j=S_BLOCKS),
+                        in_=queries[b].rearrange("(j p) k -> p j k", p=P),
+                    )
                 nc.sync.dma_start(
                     out=r_raw[h * T_CHUNKS + c][:],
                     in_=R[h, c * T_CHUNK : (c + 1) * T_CHUNK, :].rearrange("(p j) k -> p (j k)", j=ROWS),
@@ -118,44 +120,48 @@ def tile_relativepositionsdpa_pa_kernel(tc, queries, v_bias, R, out):
                 nc.scalar.copy(out=grouped_words[:, :, g, :], in_=flip[:].rearrange("p (f n) -> p n f", f=4))
             nc.vector.quantize_mx(out=r_codes[:, i, :].bitcast(FP8X4), scales=r_scales[:, i, :], in_=grouped[:])
 
-        def multiply(h, c):
-            i = h * T_CHUNKS + c
-            for b in range(h, BATCH, HEADS):
-                for j in range(S_BLOCKS):
-                    acc = psum.tile([P, T_CHUNK], F32, tag="acc")
-                    nc.tensor.matmul_mx(
-                        out=acc[:],
-                        lhsT=q_codes[:, b, j * P : (j + 1) * P].bitcast(FP8X4),
-                        lhsT_scale=q_scales[:, b, j * P : (j + 1) * P],
-                        rhs=r_codes[:, i, :].bitcast(FP8X4),
-                        rhs_scale=r_scales[:, i, :],
-                        start=True,
-                        stop=True,
-                    )
-                    dst = out_rows[b * S_BLOCKS + j][:, PAD + c * T_CHUNK : PAD + (c + 1) * T_CHUNK]
-                    if j == 0:
-                        nc.vector.tensor_copy(out=dst, in_=acc[:])
-                    else:
-                        nc.scalar.copy(out=dst, in_=acc[:])
-
-        def store(b):
-            flat = out[b].rearrange("s t -> (s t)")
-            first = out_rows[b * S_BLOCKS]
-            cut = flat[0 : P * WIDE].rearrange("(p w) -> p w", w=WIDE)
-            nc.sync.dma_start(out=cut[:, 0 : WIDE - DROP], in_=first[:, PAD - 1 + DROP : PAD + T])
-            nc.sync.dma_start(out=cut[15 : P - 1, WIDE - DROP : WIDE], in_=first[16:P, PAD - 1 : PAD - 1 + DROP])
-            nc.sync.dma_start(out=cut[0:15, WIDE - DROP : WIDE], in_=first[1:16, PAD - 1 : PAD - 1 + DROP])
-            second = out_rows[b * S_BLOCKS + 1]
-            nc.sync.dma_start(
-                out=flat[P * WIDE - DROP : S * T].rearrange("(p w) -> p w", w=WIDE),
-                in_=second[:, PAD - 1 : PAD + T],
-            )
-
-        for h in range(HEADS):
-            for b in range(h, BATCH, HEADS):
-                prepare_queries(b)
+        def row_block(b, j):
+            h = b % HEADS
+            rows = out_rows[b * S_BLOCKS + j]
             for c in range(T_CHUNKS):
-                prepare_table(h * T_CHUNKS + c)
-                multiply(h, c)
-            for b in range(h, BATCH, HEADS):
-                store(b)
+                i = h * T_CHUNKS + c
+                acc = psum.tile([P, T_CHUNK], F32, tag="acc")
+                nc.tensor.matmul_mx(
+                    out=acc[:],
+                    lhsT=q_codes[:, b, j * P : (j + 1) * P].bitcast(FP8X4),
+                    lhsT_scale=q_scales[:, b, j * P : (j + 1) * P],
+                    rhs=r_codes[:, i, :].bitcast(FP8X4),
+                    rhs_scale=r_scales[:, i, :],
+                    start=True,
+                    stop=True,
+                )
+                dst = rows[:, PAD + c * T_CHUNK : PAD + (c + 1) * T_CHUNK]
+                if c % 2 == 0:
+                    nc.vector.tensor_copy(out=dst, in_=acc[:])
+                else:
+                    nc.scalar.copy(out=dst, in_=acc[:])
+            flat = out[b].rearrange("s t -> (s t)")
+            if j == 0:
+                cut = flat[0 : P * WIDE].rearrange("(p w) -> p w", w=WIDE)
+                nc.sync.dma_start(out=cut[:, 0 : WIDE - DROP], in_=rows[:, PAD - 1 + DROP : PAD + T])
+                nc.sync.dma_start(out=cut[15 : P - 1, WIDE - DROP : WIDE], in_=rows[16:P, PAD - 1 : PAD - 1 + DROP])
+                nc.sync.dma_start(out=cut[0:15, WIDE - DROP : WIDE], in_=rows[1:16, PAD - 1 : PAD - 1 + DROP])
+            else:
+                nc.sync.dma_start(
+                    out=flat[P * WIDE - DROP : S * T].rearrange("(p w) -> p w", w=WIDE),
+                    in_=rows[:, PAD - 1 : PAD + T],
+                )
+
+        def prepare(h, step):
+            if step < SEQS:
+                prepare_queries(step * HEADS + h)
+            prepare_table(h * T_CHUNKS + step)
+
+        assert SEQS * S_BLOCKS == T_CHUNKS
+        for step in range(T_CHUNKS):
+            prepare(0, step)
+        for h in range(HEADS):
+            for step in range(T_CHUNKS):
+                row_block((step // S_BLOCKS) * HEADS + h, step % S_BLOCKS)
+                if h + 1 < HEADS:
+                    prepare(h + 1, step)

@@ -27,6 +27,7 @@ ROWS = T_CHUNK // P
 PAD = 8
 WIDE = T + 1
 DROP = S
+GROUP = 2
 
 FLOPS = 2 * BATCH * S * T * K
 BYTES = 2 * (BATCH * S * K + HEADS * K + HEADS * T * K) + 4 * BATCH * S * T
@@ -51,13 +52,12 @@ def tile_relativepositionsdpa_pa_kernel(tc, queries, v_bias, R, out):
         q_raw = [keep.tile([P, S_BLOCKS * K], BF16, name="q_raw%d" % b) for b in range(BATCH)]
         r_raw = [keep.tile([P, ROWS * K], BF16, name="r_raw%d" % i) for i in range(HEADS * T_CHUNKS)]
         for h in range(HEADS):
+            for b in range(h, BATCH, HEADS):
+                nc.sync.dma_start(
+                    out=q_raw[b][:].rearrange("p (j k) -> p j k", j=S_BLOCKS),
+                    in_=queries[b].rearrange("(j p) k -> p j k", p=P),
+                )
             for c in range(T_CHUNKS):
-                if c < SEQS:
-                    b = c * HEADS + h
-                    nc.sync.dma_start(
-                        out=q_raw[b][:].rearrange("p (j k) -> p j k", j=S_BLOCKS),
-                        in_=queries[b].rearrange("(j p) k -> p j k", p=P),
-                    )
                 nc.sync.dma_start(
                     out=r_raw[h * T_CHUNKS + c][:],
                     in_=R[h, c * T_CHUNK : (c + 1) * T_CHUNK, :].rearrange("(p j) k -> p (j k)", j=ROWS),
@@ -120,10 +120,10 @@ def tile_relativepositionsdpa_pa_kernel(tc, queries, v_bias, R, out):
                 nc.scalar.copy(out=grouped_words[:, :, g, :], in_=flip[:].rearrange("p (f n) -> p n f", f=4))
             nc.vector.quantize_mx(out=r_codes[:, i, :].bitcast(FP8X4), scales=r_scales[:, i, :], in_=grouped[:])
 
-        def row_block(b, j):
+        def products(b, j, g):
             h = b % HEADS
             rows = out_rows[b * S_BLOCKS + j]
-            for c in range(T_CHUNKS):
+            for c in range(g * GROUP, (g + 1) * GROUP):
                 i = h * T_CHUNKS + c
                 acc = psum.tile([P, T_CHUNK], F32, tag="acc")
                 nc.tensor.matmul_mx(
@@ -140,28 +140,26 @@ def tile_relativepositionsdpa_pa_kernel(tc, queries, v_bias, R, out):
                     nc.vector.tensor_copy(out=dst, in_=acc[:])
                 else:
                     nc.scalar.copy(out=dst, in_=acc[:])
+            lo = 1 + g * GROUP * T_CHUNK if g > 0 else 0
+            hi = 1 + (g + 1) * GROUP * T_CHUNK
             flat = out[b].rearrange("s t -> (s t)")
             if j == 0:
                 cut = flat[0 : P * WIDE].rearrange("(p w) -> p w", w=WIDE)
-                nc.sync.dma_start(out=cut[:, 0 : WIDE - DROP], in_=rows[:, PAD - 1 + DROP : PAD + T])
-                nc.sync.dma_start(out=cut[15 : P - 1, WIDE - DROP : WIDE], in_=rows[16:P, PAD - 1 : PAD - 1 + DROP])
-                nc.sync.dma_start(out=cut[0:15, WIDE - DROP : WIDE], in_=rows[1:16, PAD - 1 : PAD - 1 + DROP])
+                if lo == 0:
+                    nc.sync.dma_start(out=cut[15 : P - 1, WIDE - DROP : WIDE], in_=rows[16:P, PAD - 1 : PAD - 1 + DROP])
+                    nc.sync.dma_start(out=cut[0:15, WIDE - DROP : WIDE], in_=rows[1:16, PAD - 1 : PAD - 1 + DROP])
+                    lo = DROP
+                nc.sync.dma_start(out=cut[:, lo - DROP : hi - DROP], in_=rows[:, PAD - 1 + lo : PAD - 1 + hi])
             else:
-                nc.sync.dma_start(
-                    out=flat[P * WIDE - DROP : S * T].rearrange("(p w) -> p w", w=WIDE),
-                    in_=rows[:, PAD - 1 : PAD + T],
-                )
+                cut = flat[P * WIDE - DROP : S * T].rearrange("(p w) -> p w", w=WIDE)
+                nc.sync.dma_start(out=cut[:, lo:hi], in_=rows[:, PAD - 1 + lo : PAD - 1 + hi])
 
-        def prepare(h, step):
-            if step < SEQS:
-                prepare_queries(step * HEADS + h)
-            prepare_table(h * T_CHUNKS + step)
-
-        assert SEQS * S_BLOCKS == T_CHUNKS
-        for step in range(T_CHUNKS):
-            prepare(0, step)
         for h in range(HEADS):
-            for step in range(T_CHUNKS):
-                row_block((step // S_BLOCKS) * HEADS + h, step % S_BLOCKS)
-                if h + 1 < HEADS:
-                    prepare(h + 1, step)
+            for b in range(h, BATCH, HEADS):
+                prepare_queries(b)
+            for g in range(T_CHUNKS // GROUP):
+                for c in range(g * GROUP, (g + 1) * GROUP):
+                    prepare_table(h * T_CHUNKS + c)
+                for b in range(h, BATCH, HEADS):
+                    for j in range(S_BLOCKS):
+                        products(b, j, g)

@@ -28,6 +28,7 @@ PAD = 8
 WIDE = T + 1
 DROP = S
 GROUP = 2
+SLICES = HEADS * T_CHUNKS
 
 FLOPS = 2 * BATCH * S * T * K
 BYTES = 2 * (BATCH * S * K + HEADS * K + HEADS * T * K) + 4 * BATCH * S * T
@@ -39,6 +40,7 @@ def tile_relativepositionsdpa_pa_kernel(tc, queries, v_bias, R, out):
         keep = ctx.enter_context(tc.tile_pool(name="keep", bufs=1))
         stage = ctx.enter_context(tc.tile_pool(name="stage", bufs=3))
         psum = ctx.enter_context(tc.psum_pool(name="psum", bufs=4))
+        ctx.enter_context(tc.manual_schedule())
 
         ident = keep.tile([P, P], F32)
         make_identity(nc, ident[:])
@@ -50,18 +52,19 @@ def tile_relativepositionsdpa_pa_kernel(tc, queries, v_bias, R, out):
 
         nc.sync.dma_start(out=bias_rows[0:HEADS, :], in_=v_bias.rearrange("o h i k -> (o h i) k"))
         q_raw = [keep.tile([P, S_BLOCKS * K], BF16, name="q_raw%d" % b) for b in range(BATCH)]
-        r_raw = [keep.tile([P, ROWS * K], BF16, name="r_raw%d" % i) for i in range(HEADS * T_CHUNKS)]
-        for h in range(HEADS):
-            for b in range(h, BATCH, HEADS):
+        r_raw = [keep.tile([P, ROWS * K], BF16, name="r_raw%d" % i) for i in range(SLICES)]
+        for i in range(SLICES):
+            h, c = i // T_CHUNKS, i % T_CHUNKS
+            if c < SEQS:
+                b = c * HEADS + h
                 nc.sync.dma_start(
                     out=q_raw[b][:].rearrange("p (j k) -> p j k", j=S_BLOCKS),
                     in_=queries[b].rearrange("(j p) k -> p j k", p=P),
                 )
-            for c in range(T_CHUNKS):
-                nc.sync.dma_start(
-                    out=r_raw[h * T_CHUNKS + c][:],
-                    in_=R[h, c * T_CHUNK : (c + 1) * T_CHUNK, :].rearrange("(p j) k -> p (j k)", j=ROWS),
-                )
+            nc.sync.dma_start(
+                out=r_raw[i][:],
+                in_=R[h, c * T_CHUNK : (c + 1) * T_CHUNK, :].rearrange("(p j) k -> p (j k)", j=ROWS),
+            )
 
         bias_sb = keep.tile([P, HEADS * PACK], BF16)
         bias_t = psum.tile([P, 2 * P], F32, tag="flip")
@@ -74,10 +77,10 @@ def tile_relativepositionsdpa_pa_kernel(tc, queries, v_bias, R, out):
 
         q_codes = keep.tile([P, BATCH, S], U32, align_bytes=64)
         q_scales = keep.tile([P, BATCH, S], U8, align_bytes=64)
-        r_codes = keep.tile([P, HEADS * T_CHUNKS, T_CHUNK], U32, align_bytes=64)
-        r_scales = keep.tile([P, HEADS * T_CHUNKS, T_CHUNK], U8, align_bytes=64)
+        r_codes = keep.tile([P, SLICES, T_CHUNK], U32, align_bytes=64)
+        r_scales = keep.tile([P, SLICES, T_CHUNK], U8, align_bytes=64)
 
-        def prepare_queries(b):
+        def turn_queries(b):
             h = b % HEADS
             words = q_raw[b][:].bitcast(F32)
             flip = psum.tile([P, 2 * S], F32, tag="flip")
@@ -102,9 +105,9 @@ def tile_relativepositionsdpa_pa_kernel(tc, queries, v_bias, R, out):
                 op0=MULT,
                 op1=ADD,
             )
-            nc.vector.quantize_mx(out=q_codes[:, b, :].bitcast(FP8X4), scales=q_scales[:, b, :], in_=q_v[:])
+            return q_v
 
-        def prepare_table(i):
+        def turn_table(i):
             words = r_raw[i][:].bitcast(F32)
             grouped = stage.tile([P, T_CHUNK * PACK], BF16, align_bytes=64)
             grouped_words = grouped[:].bitcast(F32).rearrange("p (n g f) -> p n g f", g=2, f=4)
@@ -118,48 +121,64 @@ def tile_relativepositionsdpa_pa_kernel(tc, queries, v_bias, R, out):
                         ident[:],
                     )
                 nc.scalar.copy(out=grouped_words[:, :, g, :], in_=flip[:].rearrange("p (f n) -> p n f", f=4))
+            return grouped
+
+        def turn(i):
+            h, c = i // T_CHUNKS, i % T_CHUNKS
+            q_v = turn_queries(c * HEADS + h) if c < SEQS else None
+            return q_v, turn_table(i)
+
+        def quantise(i, turned):
+            h, c = i // T_CHUNKS, i % T_CHUNKS
+            q_v, grouped = turned
+            if c < SEQS:
+                b = c * HEADS + h
+                nc.vector.quantize_mx(out=q_codes[:, b, :].bitcast(FP8X4), scales=q_scales[:, b, :], in_=q_v[:])
             nc.vector.quantize_mx(out=r_codes[:, i, :].bitcast(FP8X4), scales=r_scales[:, i, :], in_=grouped[:])
 
-        def products(b, j, g):
+        def products(b, g):
             h = b % HEADS
-            rows = out_rows[b * S_BLOCKS + j]
-            for c in range(g * GROUP, (g + 1) * GROUP):
-                i = h * T_CHUNKS + c
-                acc = psum.tile([P, T_CHUNK], F32, tag="acc")
-                nc.tensor.matmul_mx(
-                    out=acc[:],
-                    lhsT=q_codes[:, b, j * P : (j + 1) * P].bitcast(FP8X4),
-                    lhsT_scale=q_scales[:, b, j * P : (j + 1) * P],
-                    rhs=r_codes[:, i, :].bitcast(FP8X4),
-                    rhs_scale=r_scales[:, i, :],
-                    start=True,
-                    stop=True,
-                )
-                dst = rows[:, PAD + c * T_CHUNK : PAD + (c + 1) * T_CHUNK]
-                if c % 2 == 0:
-                    nc.vector.tensor_copy(out=dst, in_=acc[:])
-                else:
-                    nc.scalar.copy(out=dst, in_=acc[:])
             lo = 1 + g * GROUP * T_CHUNK if g > 0 else 0
             hi = 1 + (g + 1) * GROUP * T_CHUNK
             flat = out[b].rearrange("s t -> (s t)")
-            if j == 0:
-                cut = flat[0 : P * WIDE].rearrange("(p w) -> p w", w=WIDE)
-                if lo == 0:
-                    nc.sync.dma_start(out=cut[15 : P - 1, WIDE - DROP : WIDE], in_=rows[16:P, PAD - 1 : PAD - 1 + DROP])
-                    nc.sync.dma_start(out=cut[0:15, WIDE - DROP : WIDE], in_=rows[1:16, PAD - 1 : PAD - 1 + DROP])
-                    lo = DROP
-                nc.sync.dma_start(out=cut[:, lo - DROP : hi - DROP], in_=rows[:, PAD - 1 + lo : PAD - 1 + hi])
-            else:
-                cut = flat[P * WIDE - DROP : S * T].rearrange("(p w) -> p w", w=WIDE)
-                nc.sync.dma_start(out=cut[:, lo:hi], in_=rows[:, PAD - 1 + lo : PAD - 1 + hi])
-
-        for h in range(HEADS):
-            for b in range(h, BATCH, HEADS):
-                prepare_queries(b)
-            for g in range(T_CHUNKS // GROUP):
+            for j in range(S_BLOCKS):
+                rows = out_rows[b * S_BLOCKS + j]
                 for c in range(g * GROUP, (g + 1) * GROUP):
-                    prepare_table(h * T_CHUNKS + c)
-                for b in range(h, BATCH, HEADS):
-                    for j in range(S_BLOCKS):
-                        products(b, j, g)
+                    i = h * T_CHUNKS + c
+                    acc = psum.tile([P, T_CHUNK], F32, tag="acc")
+                    nc.tensor.matmul_mx(
+                        out=acc[:],
+                        lhsT=q_codes[:, b, j * P : (j + 1) * P].bitcast(FP8X4),
+                        lhsT_scale=q_scales[:, b, j * P : (j + 1) * P],
+                        rhs=r_codes[:, i, :].bitcast(FP8X4),
+                        rhs_scale=r_scales[:, i, :],
+                        start=True,
+                        stop=True,
+                    )
+                    dst = rows[:, PAD + c * T_CHUNK : PAD + (c + 1) * T_CHUNK]
+                    if c % 2 == 0:
+                        nc.vector.tensor_copy(out=dst, in_=acc[:])
+                    else:
+                        nc.scalar.copy(out=dst, in_=acc[:])
+                if j == 0:
+                    cut = flat[0 : P * WIDE].rearrange("(p w) -> p w", w=WIDE)
+                    first = max(lo, DROP)
+                    nc.sync.dma_start(out=cut[:, first - DROP : hi - DROP], in_=rows[:, PAD - 1 + first : PAD - 1 + hi])
+                    if lo == 0:
+                        nc.sync.dma_start(out=cut[15 : P - 1, WIDE - DROP : WIDE], in_=rows[16:P, PAD - 1 : PAD - 1 + DROP])
+                        nc.sync.dma_start(out=cut[0:15, WIDE - DROP : WIDE], in_=rows[1:16, PAD - 1 : PAD - 1 + DROP])
+                else:
+                    cut = flat[P * WIDE - DROP : S * T].rearrange("(p w) -> p w", w=WIDE)
+                    nc.sync.dma_start(out=cut[:, lo:hi], in_=rows[:, PAD - 1 + lo : PAD - 1 + hi])
+
+        assert SEQS == GROUP
+        for i in range(GROUP):
+            quantise(i, turn(i))
+        for i in range(SLICES):
+            h, g, n = i // T_CHUNKS, (i % T_CHUNKS) // GROUP, i % GROUP
+            ahead = i + GROUP
+            if ahead < SLICES:
+                turned = turn(ahead)
+            products(n * HEADS + h, g)
+            if ahead < SLICES:
+                quantise(ahead, turned)

from contextlib import ExitStack

import concourse.mybir as mybir
from concourse.masks import make_identity

F32 = mybir.dt.float32
BF16 = mybir.dt.bfloat16
U32 = mybir.dt.uint32
U8 = mybir.dt.uint8
FP8X4 = mybir.dt.float8_e4m3fn_x4
MULT = mybir.AluOpType.mult
ADD = mybir.AluOpType.add

P = 128
HEADS = 2
SEQS = 2
BATCH = SEQS * HEADS
S = 256
T = 2048
K = 512
PACK = 4
WORDS = K // 2
S_BLOCKS = S // P
T_CHUNK = 512
T_CHUNKS = T // T_CHUNK
ROWS = T_CHUNK // P
PAD = 8
WIDE = T + 1
DROP = S
GROUP = 2
SLICES = HEADS * T_CHUNKS

FLOPS = 2 * BATCH * S * T * K
BYTES = 2 * (BATCH * S * K + HEADS * K + HEADS * T * K) + 4 * BATCH * S * T


def tile_relativepositionsdpa_pa_kernel(tc, queries, v_bias, R, out):
    nc = tc.nc
    with ExitStack() as ctx:
        keep = ctx.enter_context(tc.tile_pool(name="keep", bufs=1))
        stage = ctx.enter_context(tc.tile_pool(name="stage", bufs=3))
        psum = ctx.enter_context(tc.psum_pool(name="psum", bufs=4))
        ctx.enter_context(tc.manual_schedule())

        ident = keep.tile([P, P], F32)
        make_identity(nc, ident[:])
        bias_rows = keep.tile([P, K], BF16)
        nc.vector.memset(bias_rows[:], 0.0)
        out_rows = [keep.tile([P, PAD + T], F32, name="out_rows%d" % i) for i in range(BATCH * S_BLOCKS)]
        for rows in out_rows:
            nc.vector.memset(rows[:, 0:PAD], 0.0)

        nc.sync.dma_start(out=bias_rows[0:HEADS, :], in_=v_bias.rearrange("o h i k -> (o h i) k"))
        q_raw = [keep.tile([P, S_BLOCKS * K], BF16, name="q_raw%d" % b) for b in range(BATCH)]
        r_raw = [keep.tile([P, ROWS * K], BF16, name="r_raw%d" % i) for i in range(SLICES)]
        for i in range(SLICES):
            h, c = i // T_CHUNKS, i % T_CHUNKS
            if c < SEQS:
                b = c * HEADS + h
                nc.sync.dma_start(
                    out=q_raw[b][:].rearrange("p (j k) -> p j k", j=S_BLOCKS),
                    in_=queries[b].rearrange("(j p) k -> p j k", p=P),
                )
            nc.sync.dma_start(
                out=r_raw[i][:],
                in_=R[h, c * T_CHUNK : (c + 1) * T_CHUNK, :].rearrange("(p j) k -> p (j k)", j=ROWS),
            )

        bias_sb = keep.tile([P, HEADS * PACK], BF16)
        bias_t = psum.tile([P, 2 * P], F32, tag="flip")
        for u in range(2):
            nc.tensor.transpose(bias_t[:, u * P : (u + 1) * P], bias_rows[:].bitcast(F32)[:, u * P : (u + 1) * P], ident[:])
        nc.vector.tensor_copy(
            out=bias_sb[:].bitcast(F32).rearrange("p (h u) -> p h u", u=2),
            in_=bias_t[:].rearrange("p (u s) -> p s u", u=2)[:, 0:HEADS, :],
        )

        q_codes = keep.tile([P, BATCH, S], U32, align_bytes=64)
        q_scales = keep.tile([P, BATCH, S], U8, align_bytes=64)
        r_codes = keep.tile([P, SLICES, T_CHUNK], U32, align_bytes=64)
        r_scales = keep.tile([P, SLICES, T_CHUNK], U8, align_bytes=64)

        def turn_queries(b):
            h = b % HEADS
            words = q_raw[b][:].bitcast(F32)
            flip = psum.tile([P, 2 * S], F32, tag="flip")
            for u in range(2):
                for j in range(S_BLOCKS):
                    nc.tensor.transpose(
                        flip[:, u * S + j * P : u * S + (j + 1) * P],
                        words[:, j * WORDS + u * P : j * WORDS + (u + 1) * P],
                        ident[:],
                    )
            q_pairs = stage.tile([P, S * PACK], BF16)
            nc.scalar.copy(
                out=q_pairs[:].bitcast(F32).rearrange("p (s u) -> p s u", u=2),
                in_=flip[:].rearrange("p (u s) -> p s u", u=2),
            )
            q_v = stage.tile([P, S * PACK], BF16, align_bytes=64)
            nc.vector.scalar_tensor_tensor(
                out=q_v[:].rearrange("p (s t) -> p s t", t=PACK),
                in0=q_pairs[:].rearrange("p (s t) -> p s t", t=PACK),
                scalar=K**-0.5,
                in1=bias_sb[:, h * PACK : (h + 1) * PACK].unsqueeze(1).to_broadcast([P, S, PACK]),
                op0=MULT,
                op1=ADD,
            )
            return q_v

        def turn_table(i):
            words = r_raw[i][:].bitcast(F32)
            grouped = stage.tile([P, T_CHUNK * PACK], BF16, align_bytes=64)
            grouped_words = grouped[:].bitcast(F32).rearrange("p (n g f) -> p n g f", g=2, f=4)
            for g in range(2):
                flip = psum.tile([P, 4 * P], F32, tag="flip")
                for f in range(4):
                    j, u = 2 * g + f // 2, f % 2
                    nc.tensor.transpose(
                        flip[:, f * P : (f + 1) * P],
                        words[:, j * WORDS + u * P : j * WORDS + (u + 1) * P],
                        ident[:],
                    )
                nc.scalar.copy(out=grouped_words[:, :, g, :], in_=flip[:].rearrange("p (f n) -> p n f", f=4))
            return grouped

        def turn(i):
            h, c = i // T_CHUNKS, i % T_CHUNKS
            q_v = turn_queries(c * HEADS + h) if c < SEQS else None
            return q_v, turn_table(i)

        def quantise(i, turned):
            h, c = i // T_CHUNKS, i % T_CHUNKS
            q_v, grouped = turned
            if c < SEQS:
                b = c * HEADS + h
                nc.vector.quantize_mx(out=q_codes[:, b, :].bitcast(FP8X4), scales=q_scales[:, b, :], in_=q_v[:])
            nc.vector.quantize_mx(out=r_codes[:, i, :].bitcast(FP8X4), scales=r_scales[:, i, :], in_=grouped[:])

        def products(b, g):
            h = b % HEADS
            lo = 1 + g * GROUP * T_CHUNK if g > 0 else 0
            hi = 1 + (g + 1) * GROUP * T_CHUNK
            flat = out[b].rearrange("s t -> (s t)")
            for j in range(S_BLOCKS):
                rows = out_rows[b * S_BLOCKS + j]
                for c in range(g * GROUP, (g + 1) * GROUP):
                    i = h * T_CHUNKS + c
                    acc = psum.tile([P, T_CHUNK], F32, tag="acc")
                    nc.tensor.matmul_mx(
                        out=acc[:],
                        lhsT=q_codes[:, b, j * P : (j + 1) * P].bitcast(FP8X4),
                        lhsT_scale=q_scales[:, b, j * P : (j + 1) * P],
                        rhs=r_codes[:, i, :].bitcast(FP8X4),
                        rhs_scale=r_scales[:, i, :],
                        start=True,
                        stop=True,
                    )
                    dst = rows[:, PAD + c * T_CHUNK : PAD + (c + 1) * T_CHUNK]
                    if c % 2 == 0:
                        nc.vector.tensor_copy(out=dst, in_=acc[:])
                    else:
                        nc.scalar.copy(out=dst, in_=acc[:])
                if j == 0:
                    cut = flat[0 : P * WIDE].rearrange("(p w) -> p w", w=WIDE)
                    first = max(lo, DROP)
                    nc.sync.dma_start(out=cut[:, first - DROP : hi - DROP], in_=rows[:, PAD - 1 + first : PAD - 1 + hi])
                    if lo == 0:
                        nc.sync.dma_start(out=cut[15 : P - 1, WIDE - DROP : WIDE], in_=rows[16:P, PAD - 1 : PAD - 1 + DROP])
                        nc.sync.dma_start(out=cut[0:15, WIDE - DROP : WIDE], in_=rows[1:16, PAD - 1 : PAD - 1 + DROP])
                else:
                    cut = flat[P * WIDE - DROP : S * T].rearrange("(p w) -> p w", w=WIDE)
                    nc.sync.dma_start(out=cut[:, lo:hi], in_=rows[:, PAD - 1 + lo : PAD - 1 + hi])

        assert SEQS == GROUP
        for i in range(GROUP):
            quantise(i, turn(i))
        for i in range(SLICES):
            h, g, n = i // T_CHUNKS, (i % T_CHUNKS) // GROUP, i % GROUP
            ahead = i + GROUP
            if ahead < SLICES:
                turned = turn(ahead)
            products(n * HEADS + h, g)
            if ahead < SLICES:
                quantise(ahead, turned)
